import numpy as np
import ml_dtypes


def mxq(x, axis, fmt="e4m3"):
    dtype, down = {"e4m3": (ml_dtypes.float8_e4m3fn, 7), "e5m2": (ml_dtypes.float8_e5m2, 14)}[fmt]
    v = np.moveaxis(np.asarray(x, np.float32).astype(ml_dtypes.bfloat16).astype(np.float64), axis, -1)
    blocks = v.reshape(v.shape[:-1] + (-1, 32))
    amax = np.abs(blocks).max(-1, keepdims=True)
    byte = np.maximum(np.where(amax > 0, np.frexp(amax)[1] - 1 + 127, 0) - down, 1)
    scale = np.exp2(byte - 127.0)
    codes = (blocks / scale).astype(np.float32).astype(dtype).astype(np.float64)
    return np.moveaxis((codes * scale).reshape(v.shape), -1, axis)


WIDE = False


def mx_kscale(k):
    if not WIDE:
        return np.ones(k)
    levels = np.array([10, -10, 5, -5, 0])
    if k % 512:
        return np.exp2(np.random.permutation(np.resize(levels, k // 32))).repeat(32)
    a = np.empty((k // 512, 16))
    for p in range(k // 512):
        a[p, :8] = np.random.permutation(np.resize(levels, 8))
        for g in range(8):
            far = levels[np.abs(levels - a[p, g]) >= 10]
            a[p, g + 8] = far[np.random.randint(len(far))]
    return np.exp2(a.ravel()).repeat(32)


BF16 = ml_dtypes.bfloat16


def bf(x):
    return np.asarray(x, np.float32).astype(BF16)


def f64(x):
    return np.asarray(x).astype(np.float64)


N, CIN, COUT, V, T, S = 1, 512, 128, 32, 128, 16
EPS = 1e-5
KG = S * V


def setup_inputs():
    r = np.random.standard_normal
    c = mx_kscale(CIN)
    g = mx_kscale(KG).reshape(S, V)
    return {"ada_A": bf(r((N, CIN, V, V)) * c[None, :, None, None]),
            "ada_w": bf(r((S, COUT, CIN)) / np.sqrt(CIN) / c),
            "ada_b": bf(r((S, COUT)) * 0.3),
            "PA": bf(r((S, V, V)) * 2.0 / np.sqrt(KG) * g[:, None, :]),
            "feat": bf(r((S, N, COUT, V, T)) / g[:, None, None, :, None]),
            "bn_gamma": bf(1.0 + 0.1 * r(COUT)),
            "bn_beta": bf(0.3 * r(COUT)),
            "bn_mean": bf(0.3 * r(COUT)),
            "bn_var": bf(np.abs(r(COUT)) + 1.0),
            "res": bf(r((N, COUT, V, T)) * 0.9)}


def reference(ada_A, ada_w, ada_b, PA, feat, bn_gamma, bn_beta, bn_mean, bn_var, res):
    wq = mxq(f64(ada_w).reshape(S * COUT, CIN), 1, "e4m3")
    aq = mxq(f64(ada_A).reshape(N, CIN, V * V), 1, "e4m3")
    adaA = (wq @ aq).reshape(N, S, COUT, V, V).transpose(1, 0, 2, 3, 4) + f64(ada_b)[:, None, :, None, None]
    A_full = adaA * f64(PA)[:, None, None, :, :]
    Ag = A_full.transpose(1, 2, 3, 0, 4).reshape(N, COUT, V, KG)
    Fg = f64(feat).transpose(1, 2, 0, 3, 4).reshape(N, COUT, KG, T)
    y = mxq(Ag, 3, "e4m3") @ mxq(Fg, 2, "e4m3")
    scale = f64(bn_gamma) / np.sqrt(f64(bn_var) + EPS)
    z = (y - f64(bn_mean)[:, None, None]) * scale[:, None, None] + f64(bn_beta)[:, None, None]
    return np.maximum(z + f64(res), 0.0)

@@ -1,0 +1,340 @@
+from contextlib import ExitStack
+
+import concourse.mybir as mybir
+from concourse.masks import make_identity
+
+F32 = mybir.dt.float32
+BF16 = mybir.dt.bfloat16
+I32 = mybir.dt.int32
+U8 = mybir.dt.uint8
+FP8X4 = mybir.dt.float8_e4m3fn_x4
+ALU = mybir.AluOpType
+ACT = mybir.ActivationFunctionType
+
+P = 128
+NS = 16
+NO = 128
+NV = 32
+NT = 128
+EPS = 1e-5
+CH = 8
+NCH = NO // CH
+OB = 32
+NBLK = NO // OB
+NZ = 4
+V_SHARE = (2, 1)
+G_SHARE = (2,)
+MID = F32
+
+FLOPS = 2 * (NS * NO) * 512 * (NV * NV) + 2 * NO * NV * (NS * NV) * NT
+
+
+def tile_multiscale_gcn_pa_kernel(tc, ada_A, ada_w, ada_b, PA, feat, bn_gamma, bn_beta, bn_mean, bn_var, res, out):
+    nc = tc.nc
+    with ExitStack() as ctx:
+        const = ctx.enter_context(tc.tile_pool(name="const", bufs=1))
+        rawp = ctx.enter_context(tc.tile_pool(name="rawp", bufs=6))
+        ilp = ctx.enter_context(tc.tile_pool(name="ilp", bufs=2))
+        fcp = ctx.enter_context(tc.tile_pool(name="fcp", bufs=6))
+        xp = ctx.enter_context(tc.tile_pool(name="xp", bufs=2))
+        aip = ctx.enter_context(tc.tile_pool(name="aip", bufs=3))
+        finp = ctx.enter_context(tc.tile_pool(name="finp", bufs=3))
+        psum = ctx.enter_context(tc.psum_pool(name="psum", bufs=2))
+        with tc.manual_schedule():
+            zcs = []
+            for i in range(NZ):
+                z = const.tile([P, CH, 160], I32, name="zc%d" % i, tag="zc%d" % i, align_bytes=64)
+                nc.vector.memset(z[:], 0)
+                zcs.append(z)
+            identF = const.tile([P, P], F32, name="identF", tag="identF")
+            make_identity(nc, identF[:])
+            identM = identF
+            ones = const.tile([P, P], BF16, name="ones", tag="ones")
+            nc.gpsimd.memset(ones[:], 1.0)
+            bnrow = const.tile([P, 4 * NO], BF16, name="bnrow", tag="bnrow")
+            nc.gpsimd.memset(bnrow[:], 0.0)
+            warm = const.tile([P, 1], F32, name="warm", tag="warm")
+            nc.gpsimd.memset(warm[:], 1.0)
+            nc.scalar.activation(out=warm[:], in_=warm[:], func=ACT.Sqrt)
+
+            for k, vec in enumerate((bn_gamma, bn_beta, bn_mean, bn_var)):
+                nc.sync.dma_start(out=bnrow[0:1, k * NO : (k + 1) * NO], in_=vec.rearrange("(x o) -> x o", x=1))
+            rawA = rawp.tile([P, 4, NV * NV], BF16, name="rawA", tag="raw")
+            nc.sync.dma_start(out=rawA[:], in_=ada_A[0].rearrange("(p j) v w -> p j (v w)", j=4))
+            rawW = []
+            for h in range(2):
+                rw = rawp.tile([P, 8, 512], BF16, name="rawW%d" % h, tag="raw")
+                rawW.append(rw)
+                for q in range(2):
+                    s0 = 8 * h + 4 * q
+                    nc.sync.dma_start(out=rw[:, 4 * q : 4 * q + 4, :], in_=ada_w[s0 : s0 + 4].rearrange("s o i -> o s i"))
+
+            raws = {}
+
+            def ld(c):
+                if c < 0 or c >= NCH:
+                    return
+                r = rawp.tile([P, CH, 4, NT], BF16, name="raw", tag="raw")
+                raws[c] = r
+                for ol in range(CH):
+                    nc.sync.dma_start(
+                        out=r[:, ol].rearrange("p j t -> p (j t)"),
+                        in_=feat[:, 0, c * CH + ol].rearrange("s (a j) t -> s a (j t)", j=4),
+                    )
+
+            ld(0)
+            PAt = const.tile([P, P], BF16, name="PAt", tag="PAt")
+            bt = const.tile([P, NO], BF16, name="bt", tag="bt")
+            for a in range(8):
+                nc.sync.dma_start(
+                    out=PAt[a::8, :].rearrange("s (v b) -> s v b", b=4), in_=PA[:, :, 4 * a : 4 * a + 4]
+                )
+            nc.sync.dma_start(out=bt[:], in_=ada_b.unsqueeze(1).to_broadcast([NS, 8, NO]))
+            ld(1)
+            ld(2)
+            res_sb = const.tile([P, NO // 4, NT], BF16, name="res_sb", tag="res_sb")
+            nc.sync.dma_start(out=res_sb[:], in_=res[0].rearrange("(g q) v t -> (q v) g t", q=4))
+            out_v = out[0].rearrange("(g q) v t -> (q v) g t", q=4)
+
+            sc_t = const.tile([P, NO // 4], F32, name="sc_t", tag="sc_t")
+            sh_t = const.tile([P, NO // 4], F32, name="sh_t", tag="sh_t")
+
+            def bn():
+                psbn = psum.tile([P, 4 * NO], F32, name="psbn", tag="ps2", bufs=2)
+                nc.tensor.matmul(out=psbn[:], lhsT=ones[:], rhs=bnrow[:], start=True, stop=True)
+                std = const.tile([P, NO], F32, name="std", tag="std")
+                nc.scalar.activation(out=std[:], in_=psbn[:, 3 * NO : 4 * NO], func=ACT.Sqrt, bias=EPS, scale=1.0)
+                rstd = const.tile([P, NO], F32, name="rstd", tag="rstd")
+                nc.vector.reciprocal(out=rstd[:], in_=std[:])
+                scl = const.tile([P, NO], F32, name="scl", tag="scl")
+                nc.vector.tensor_tensor(out=scl[:], in0=psbn[:, 0:NO], in1=rstd[:], op=ALU.mult)
+                msc = const.tile([P, NO], F32, name="msc", tag="msc")
+                nc.vector.tensor_tensor(out=msc[:], in0=psbn[:, 2 * NO : 3 * NO], in1=scl[:], op=ALU.mult)
+                shf = const.tile([P, NO], F32, name="shf", tag="shf")
+                nc.vector.tensor_tensor(out=shf[:], in0=psbn[:, NO : 2 * NO], in1=msc[:], op=ALU.subtract)
+                for q in range(4):
+                    rows = slice(32 * q, 32 * q + 32)
+                    nc.gpsimd.tensor_copy(out=sc_t[rows, :], in_=scl[rows, q::4])
+                    nc.gpsimd.tensor_copy(out=sh_t[rows, :], in_=shf[rows, q::4])
+
+            bn()
+
+            ilA = ilp.tile([P, 8, NV, 4, 4], BF16, name="ilA", tag="il", align_bytes=64)
+            rawA_v = rawA[:].rearrange("p j (v a b) -> p a v b j", a=8, b=4)
+            for a in range(8):
+                if a < 4:
+                    nc.vector.tensor_copy(out=ilA[:, a], in_=rawA_v[:, a])
+                else:
+                    nc.scalar.copy(out=ilA[:, a], in_=rawA_v[:, a])
+            acodes = const.tile([P, 1024], I32, name="acodes", tag="acodes", align_bytes=64)
+            ascl = const.tile([P, 1024], U8, name="ascl", tag="ascl", align_bytes=64)
+            for h in range(2):
+                nc.vector.quantize_mx(
+                    out=acodes[:, 512 * h : 512 * h + 512].bitcast(FP8X4),
+                    scales=ascl[:, 512 * h : 512 * h + 512],
+                    in_=ilA[:, 4 * h : 4 * h + 4].rearrange("p a v b j -> p (a v b j)"),
+                )
+
+            ilW = const.tile([P, NBLK, NS, OB * 4], BF16, name="ilW", tag="ilW", align_bytes=64)
+            ilW_w = ilW[:].bitcast(F32)
+            for sp in range(NS // 2):
+                tpw = psum.tile([P, 4, P], F32, name="tpw", tag="tp", bufs=4)
+                for sl in range(2):
+                    s = 2 * sp + sl
+                    words = rawW[s // 8][:, s % 8, :].bitcast(F32)
+                    for u in range(2):
+                        nc.tensor.transpose(tpw[:, 2 * sl + u, :], words[:, u::2], identF[:])
+                for sl in range(2):
+                    s = 2 * sp + sl
+                    dst = ilW_w[:, :, s, :].rearrange("p b (o u) -> p b o u", u=2)
+                    src = tpw[:, 2 * sl : 2 * sl + 2, :].rearrange("p u (b o) -> p b o u", b=NBLK)
+                    if sp % 2 == 0:
+                        nc.scalar.copy(out=dst, in_=src)
+                    else:
+                        nc.vector.tensor_copy(out=dst, in_=src)
+            wcodes = const.tile([P, NS * NO], I32, name="wcodes", tag="wcodes", align_bytes=64)
+            wscl = const.tile([P, NS * NO], U8, name="wscl", tag="wscl", align_bytes=64)
+
+            def qw(b):
+                nc.vector.quantize_mx(
+                    out=wcodes[:, 512 * b : 512 * b + 512].bitcast(FP8X4),
+                    scales=wscl[:, 512 * b : 512 * b + 512],
+                    in_=ilW[:, b].rearrange("p s x -> p (s x)"),
+                )
+
+            xs = {}
+            tps = {}
+            ais = {}
+            ccs = {}
+            css = {}
+            ils = {}
+            fcs = {}
+            fss = {}
+            ps2s = {}
+            tmps = {}
+
+            def mm1(b, a):
+                if a == 0:
+                    xs[b] = xp.tile([P, NS, 8, OB], MID, name="X", tag="X")
+                if b == 0 and a % 2 == 1:
+                    ps1 = psum.tile([P, 512], MID, name="ps1b", tag="tp", bufs=4)
+                else:
+                    ps1 = psum.tile([P, 512], MID, name="ps1", tag="ps1", bufs=2)
+                nc.tensor.matmul_mx(
+                    out=ps1[:],
+                    lhsT=acodes[:, P * a : P * a + P].bitcast(FP8X4),
+                    lhsT_scale=ascl[:, P * a : P * a + P],
+                    rhs=wcodes[:, 512 * b : 512 * b + 512].bitcast(FP8X4),
+                    rhs_scale=wscl[:, 512 * b : 512 * b + 512],
+                    start=True,
+                    stop=True,
+                )
+                if b == 0 and a % 2 == 1:
+                    nc.vector.tensor_copy(out=xs[b][:, :, a, :], in_=ps1[:].rearrange("p (s o) -> p s o", o=OB))
+                else:
+                    nc.scalar.copy(out=xs[b][:, :, a, :], in_=ps1[:].rearrange("p (s o) -> p s o", o=OB))
+
+            def t2(c):
+                if c < 0 or c >= NCH:
+                    return
+                xv = xs[c // 4][:].rearrange("p s a o -> p (s a) o")
+                tps[c] = []
+                for h in range(2):
+                    tp = psum.tile([P, 4, P], MID, name="tp", tag="tp", bufs=4)
+                    tps[c].append(tp)
+                    for i in range(4):
+                        nc.tensor.transpose(tp[:, i, :], xv[:, :, (c % 4) * CH + 4 * h + i], identM[:])
+
+            def stt(c):
+                if c < 0 or c >= NCH:
+                    return
+                ai = aip.tile([P, CH * P], BF16, name="ai", tag="ai", bufs=3, align_bytes=64)
+                ais[c] = ai
+                for i in range(CH):
+                    o = c * CH + i
+                    nc.vector.scalar_tensor_tensor(
+                        out=ai[:, P * i : P * i + P],
+                        in0=tps[c][i // 4][:, i % 4, :],
+                        scalar=bt[:, o : o + 1],
+                        in1=PAt[:],
+                        op0=ALU.add,
+                        op1=ALU.mult,
+                    )
+
+            def qa(c):
+                if c < 0 or c >= NCH:
+                    return
+                cc = aip.tile([P, CH * NV], I32, name="cc", tag="cc", bufs=3, align_bytes=64)
+                cs = aip.tile([P, CH * NV], U8, name="cs", tag="cs", bufs=5, align_bytes=64)
+                ccs[c] = cc
+                css[c] = cs
+                nc.vector.quantize_mx(out=cc[:].bitcast(FP8X4), scales=cs[:], in_=ais[c][:])
+
+            def mv(c):
+                if c < 0 or c >= NCH:
+                    return
+                nc.vector.tensor_copy(out=zcs[c % NZ][:, :, 0:NV], in_=ccs[c][:].rearrange("p (a b) -> p a b", b=NV))
+
+            def il(c):
+                if c < 0 or c >= NCH:
+                    return
+                t = ilp.tile([P, CH, NT, 4], BF16, name="il", tag="il", align_bytes=64)
+                ils[c] = t
+                src = raws[c][:].rearrange("p o j t -> p o t j")
+                nv = V_SHARE[c % len(V_SHARE)]
+                ng = G_SHARE[c % len(G_SHARE)]
+                ns = CH - nv - ng
+                if ng > 0:
+                    nc.gpsimd.tensor_scalar(
+                        out=t[:, ns + nv : CH], in0=src[:, ns + nv : CH], scalar1=1.0, scalar2=0.0, op0=ALU.mult, op1=ALU.add
+                    )
+                cuts = [(ns, ns + nv)] if (nv % 2 == 0 or nv == 1) else [(ns, ns + nv - 1), (ns + nv - 1, ns + nv)]
+                for lo, hi in cuts:
+                    if hi > lo:
+                        nc.vector.tensor_copy(out=t[:, lo:hi], in_=src[:, lo:hi])
+                nc.scalar.copy(out=t[:, 0:ns], in_=src[:, 0:ns])
+
+            def qf(c):
+                if c < 0 or c >= NCH:
+                    return
+                fc = fcp.tile([P, CH * NT], I32, name="fc", tag="fc", align_bytes=64)
+                fs = fcp.tile([P, CH * NT], U8, name="fs", tag="fs", align_bytes=64)
+                fcs[c] = fc
+                fss[c] = fs
+                nc.vector.quantize_mx(
+                    out=fc[:].bitcast(FP8X4), scales=fs[:], in_=ils[c][:].rearrange("p o t j -> p (o t j)")
+                )
+
+            def mm2(c):
+                if c < 0 or c >= NCH:
+                    return
+                ps2 = psum.tile([P, 2, NT], F32, name="ps2", tag="ps2", bufs=2)
+                ps2s[c] = ps2
+                zflat = zcs[c % NZ][:].rearrange("p a b -> p (a b)")
+                for gi in range(2):
+                    for j in range(4):
+                        ol = 4 * gi + j
+                        w0 = 640 * gi + P * j
+                        nc.tensor.matmul_mx(
+                            out=ps2[:, gi, :],
+                            lhsT=zflat[:, w0 : w0 + P].bitcast(FP8X4),
+                            lhsT_scale=css[c][:, P * gi : P * gi + P],
+                            rhs=fcs[c][:, NT * ol : NT * ol + NT].bitcast(FP8X4),
+                            rhs_scale=fss[c][:, NT * ol : NT * ol + NT],
+                            start=(j == 0),
+                            stop=(j == 3),
+                        )
+
+            def fin_v(c):
+                if c < 0 or c >= NCH:
+                    return
+                tmp = finp.tile([P, 2, NT], F32, name="tmp", tag="tmp")
+                tmps[c] = tmp
+                for gi in range(2):
+                    g = 2 * c + gi
+                    nc.vector.scalar_tensor_tensor(
+                        out=tmp[:, gi, :],
+                        in0=ps2s[c][:, gi, :],
+                        scalar=sc_t[:, g : g + 1],
+                        in1=res_sb[:, g, :],
+                        op0=ALU.mult,
+                        op1=ALU.add,
+                    )
+
+            def fin_s(c):
+                if c < 0 or c >= NCH:
+                    return
+                ost = finp.tile([P, 2, NT], F32, name="ost", tag="ost")
+                for gi in range(2):
+                    g = 2 * c + gi
+                    nc.scalar.activation(
+                        out=ost[:, gi, :], in_=tmps[c][:, gi, :], func=ACT.Relu, bias=sh_t[:, g : g + 1], scale=1.0
+                    )
+                nc.sync.dma_start(out=out_v[:, 2 * c : 2 * c + 2, :], in_=ost[:])
+
+            qw(0)
+            il(0)
+            for a in range(8):
+                mm1(0, a)
+            qw(1)
+            ld(3)
+            for c in range(-2, NCH + 2):
+                ld(c + 6)
+                t2(c + 2)
+                k = c + 6
+                if 4 <= k < 4 * NBLK:
+                    mm1(k // 4, 2 * (k % 4))
+                    mm1(k // 4, 2 * (k % 4) + 1)
+                mm2(c - 1)
+                stt(c + 1)
+                fin_v(c - 2)
+                qa(c + 1)
+                if c + 1 > 0:
+                    il(c + 1)
+                mv(c + 1)
+                if c == -1:
+                    qw(2)
+                if c == 1:
+                    qw(3)
+                qf(c)
+                fin_s(c - 2)

@@ -22,8 +22,8 @@ NCH = NO // CH
 OB = 32
 NBLK = NO // OB
 NZ = 4
-V_SHARE = (2, 1)
-G_SHARE = (2,)
+V_SHARE = (4, 2, 4) * 4 + (2,) * 4
+G_SHARE = (0,)
 MID = F32
 
 FLOPS = 2 * (NS * NO) * 512 * (NV * NV) + 2 * NO * NV * (NS * NV) * NT
@@ -34,7 +34,7 @@ def tile_multiscale_gcn_pa_kernel(tc, ada_A, ada_w, ada_b, PA, feat, bn_gamma, b
     with ExitStack() as ctx:
         const = ctx.enter_context(tc.tile_pool(name="const", bufs=1))
         rawp = ctx.enter_context(tc.tile_pool(name="rawp", bufs=6))
-        ilp = ctx.enter_context(tc.tile_pool(name="ilp", bufs=2))
+        ilp = ctx.enter_context(tc.tile_pool(name="ilp", bufs=3))
         fcp = ctx.enter_context(tc.tile_pool(name="fcp", bufs=6))
         xp = ctx.enter_context(tc.tile_pool(name="xp", bufs=2))
         aip = ctx.enter_context(tc.tile_pool(name="aip", bufs=3))

@@ -22,8 +22,7 @@ NCH = NO // CH
 OB = 32
 NBLK = NO // OB
 NZ = 4
-V_SHARE = (4, 2, 4) * 4 + (2,) * 4
-G_SHARE = (0,)
+V_SHARE = (4, 2, 4) * 4 + (2, 2, 2, 4)
 MID = F32
 
 FLOPS = 2 * (NS * NO) * 512 * (NV * NV) + 2 * NO * NV * (NS * NV) * NT
@@ -38,7 +37,7 @@ def tile_multiscale_gcn_pa_kernel(tc, ada_A, ada_w, ada_b, PA, feat, bn_gamma, b
         fcp = ctx.enter_context(tc.tile_pool(name="fcp", bufs=6))
         xp = ctx.enter_context(tc.tile_pool(name="xp", bufs=2))
         aip = ctx.enter_context(tc.tile_pool(name="aip", bufs=3))
-        finp = ctx.enter_context(tc.tile_pool(name="finp", bufs=3))
+        finp = ctx.enter_context(tc.tile_pool(name="finp", bufs=4))
         psum = ctx.enter_context(tc.psum_pool(name="psum", bufs=2))
         with tc.manual_schedule():
             zcs = []
@@ -57,6 +56,13 @@ def tile_multiscale_gcn_pa_kernel(tc, ada_A, ada_w, ada_b, PA, feat, bn_gamma, b
             nc.gpsimd.memset(warm[:], 1.0)
             nc.scalar.activation(out=warm[:], in_=warm[:], func=ACT.Sqrt)
 
+            PAt = const.tile([P, P], BF16, name="PAt", tag="PAt")
+            bt = const.tile([P, NO], BF16, name="bt", tag="bt")
+            for a in range(8):
+                nc.gpsimd.dma_start(
+                    out=PAt[a::8, :].rearrange("s (v b) -> s v b", b=4), in_=PA[:, :, 4 * a : 4 * a + 4]
+                )
+            nc.gpsimd.dma_start(out=bt[:], in_=ada_b.unsqueeze(1).to_broadcast([NS, 8, NO]))
             for k, vec in enumerate((bn_gamma, bn_beta, bn_mean, bn_var)):
                 nc.sync.dma_start(out=bnrow[0:1, k * NO : (k + 1) * NO], in_=vec.rearrange("(x o) -> x o", x=1))
             rawA = rawp.tile([P, 4, NV * NV], BF16, name="rawA", tag="raw")
@@ -83,41 +89,11 @@ def tile_multiscale_gcn_pa_kernel(tc, ada_A, ada_w, ada_b, PA, feat, bn_gamma, b
                     )
 
             ld(0)
-            PAt = const.tile([P, P], BF16, name="PAt", tag="PAt")
-            bt = const.tile([P, NO], BF16, name="bt", tag="bt")
-            for a in range(8):
-                nc.sync.dma_start(
-                    out=PAt[a::8, :].rearrange("s (v b) -> s v b", b=4), in_=PA[:, :, 4 * a : 4 * a + 4]
-                )
-            nc.sync.dma_start(out=bt[:], in_=ada_b.unsqueeze(1).to_broadcast([NS, 8, NO]))
             ld(1)
             ld(2)
             res_sb = const.tile([P, NO // 4, NT], BF16, name="res_sb", tag="res_sb")
             nc.sync.dma_start(out=res_sb[:], in_=res[0].rearrange("(g q) v t -> (q v) g t", q=4))
             out_v = out[0].rearrange("(g q) v t -> (q v) g t", q=4)
-
-            sc_t = const.tile([P, NO // 4], F32, name="sc_t", tag="sc_t")
-            sh_t = const.tile([P, NO // 4], F32, name="sh_t", tag="sh_t")
-
-            def bn():
-                psbn = psum.tile([P, 4 * NO], F32, name="psbn", tag="ps2", bufs=2)
-                nc.tensor.matmul(out=psbn[:], lhsT=ones[:], rhs=bnrow[:], start=True, stop=True)
-                std = const.tile([P, NO], F32, name="std", tag="std")
-                nc.scalar.activation(out=std[:], in_=psbn[:, 3 * NO : 4 * NO], func=ACT.Sqrt, bias=EPS, scale=1.0)
-                rstd = const.tile([P, NO], F32, name="rstd", tag="rstd")
-                nc.vector.reciprocal(out=rstd[:], in_=std[:])
-                scl = const.tile([P, NO], F32, name="scl", tag="scl")
-                nc.vector.tensor_tensor(out=scl[:], in0=psbn[:, 0:NO], in1=rstd[:], op=ALU.mult)
-                msc = const.tile([P, NO], F32, name="msc", tag="msc")
-                nc.vector.tensor_tensor(out=msc[:], in0=psbn[:, 2 * NO : 3 * NO], in1=scl[:], op=ALU.mult)
-                shf = const.tile([P, NO], F32, name="shf", tag="shf")
-                nc.vector.tensor_tensor(out=shf[:], in0=psbn[:, NO : 2 * NO], in1=msc[:], op=ALU.subtract)
-                for q in range(4):
-                    rows = slice(32 * q, 32 * q + 32)
-                    nc.gpsimd.tensor_copy(out=sc_t[rows, :], in_=scl[rows, q::4])
-                    nc.gpsimd.tensor_copy(out=sh_t[rows, :], in_=shf[rows, q::4])
-
-            bn()
 
             ilA = ilp.tile([P, 8, NV, 4, 4], BF16, name="ilA", tag="il", align_bytes=64)
             rawA_v = rawA[:].rearrange("p j (v a b) -> p a v b j", a=8, b=4)
@@ -162,6 +138,27 @@ def tile_multiscale_gcn_pa_kernel(tc, ada_A, ada_w, ada_b, PA, feat, bn_gamma, b
                     in_=ilW[:, b].rearrange("p s x -> p (s x)"),
                 )
 
+            sc_t = const.tile([P, NO // 4], F32, name="sc_t", tag="sc_t")
+            sh_t = const.tile([P, NO // 4], F32, name="sh_t", tag="sh_t")
+
+            def bn():
+                psbn = psum.tile([P, 4 * NO], F32, name="psbn", tag="ps2", bufs=2)
+                nc.tensor.matmul(out=psbn[:], lhsT=ones[:], rhs=bnrow[:], start=True, stop=True)
+                std = const.tile([P, NO], F32, name="std", tag="std")
+                nc.scalar.activation(out=std[:], in_=psbn[:, 3 * NO : 4 * NO], func=ACT.Sqrt, bias=EPS, scale=1.0)
+                rstd = const.tile([P, NO], F32, name="rstd", tag="rstd")
+                nc.vector.reciprocal(out=rstd[:], in_=std[:])
+                scl = const.tile([P, NO], F32, name="scl", tag="scl")
+                nc.vector.tensor_tensor(out=scl[:], in0=psbn[:, 0:NO], in1=rstd[:], op=ALU.mult)
+                msc = const.tile([P, NO], F32, name="msc", tag="msc")
+                nc.vector.tensor_tensor(out=msc[:], in0=psbn[:, 2 * NO : 3 * NO], in1=scl[:], op=ALU.mult)
+                shf = const.tile([P, NO], F32, name="shf", tag="shf")
+                nc.vector.tensor_tensor(out=shf[:], in0=psbn[:, NO : 2 * NO], in1=msc[:], op=ALU.subtract)
+                for q in range(4):
+                    rows = slice(32 * q, 32 * q + 32)
+                    nc.gpsimd.tensor_copy(out=sc_t[rows, :], in_=scl[rows, q::4])
+                    nc.gpsimd.tensor_copy(out=sh_t[rows, :], in_=shf[rows, q::4])
+
             xs = {}
             tps = {}
             ais = {}
@@ -172,6 +169,7 @@ def tile_multiscale_gcn_pa_kernel(tc, ada_A, ada_w, ada_b, PA, feat, bn_gamma, b
             fss = {}
             ps2s = {}
             tmps = {}
+            osts = {}
 
             def mm1(b, a):
                 if a == 0:
@@ -235,65 +233,67 @@ def tile_multiscale_gcn_pa_kernel(tc, ada_A, ada_w, ada_b, PA, feat, bn_gamma, b
                     return
                 nc.vector.tensor_copy(out=zcs[c % NZ][:, :, 0:NV], in_=ccs[c][:].rearrange("p (a b) -> p a b", b=NV))
 
-            def il(c):
-                if c < 0 or c >= NCH:
-                    return
-                t = ilp.tile([P, CH, NT, 4], BF16, name="il", tag="il", align_bytes=64)
-                ils[c] = t
-                src = raws[c][:].rearrange("p o j t -> p o t j")
-                nv = V_SHARE[c % len(V_SHARE)]
-                ng = G_SHARE[c % len(G_SHARE)]
-                ns = CH - nv - ng
-                if ng > 0:
-                    nc.gpsimd.tensor_scalar(
-                        out=t[:, ns + nv : CH], in0=src[:, ns + nv : CH], scalar1=1.0, scalar2=0.0, op0=ALU.mult, op1=ALU.add
-                    )
-                cuts = [(ns, ns + nv)] if (nv % 2 == 0 or nv == 1) else [(ns, ns + nv - 1), (ns + nv - 1, ns + nv)]
-                for lo, hi in cuts:
-                    if hi > lo:
-                        nc.vector.tensor_copy(out=t[:, lo:hi], in_=src[:, lo:hi])
-                nc.scalar.copy(out=t[:, 0:ns], in_=src[:, 0:ns])
+            def cuts(c, lo, hi):
+                if c == NCH - 1:
+                    mid = (lo + hi) // 2
+                    return [(lo, mid), (mid, hi)]
+                return [(lo, hi)]
 
-            def qf(c):
+            def il_s(c):
                 if c < 0 or c >= NCH:
                     return
-                fc = fcp.tile([P, CH * NT], I32, name="fc", tag="fc", align_bytes=64)
-                fs = fcp.tile([P, CH * NT], U8, name="fs", tag="fs", align_bytes=64)
-                fcs[c] = fc
-                fss[c] = fs
+                ils[c] = ilp.tile([P, CH, NT, 4], BF16, name="il", tag="il", align_bytes=64)
+                src = raws[c][:].rearrange("p o j t -> p o t j")
+                for lo, hi in cuts(c, 0, CH - V_SHARE[c]):
+                    nc.scalar.copy(out=ils[c][:, lo:hi], in_=src[:, lo:hi])
+
+            def il_v(c):
+                if c < 0 or c >= NCH:
+                    return
+                src = raws[c][:].rearrange("p o j t -> p o t j")
+                for lo, hi in cuts(c, CH - V_SHARE[c], CH):
+                    nc.vector.tensor_copy(out=ils[c][:, lo:hi], in_=src[:, lo:hi])
+
+            def qf(c, h):
+                if c < 0 or c >= NCH:
+                    return
+                if h == 0:
+                    fcs[c] = fcp.tile([P, CH * NT], I32, name="fc", tag="fc", align_bytes=64)
+                    fss[c] = fcp.tile([P, CH * NT], U8, name="fs", tag="fs", align_bytes=64)
+                cols = slice(512 * h, 512 * h + 512)
                 nc.vector.quantize_mx(
-                    out=fc[:].bitcast(FP8X4), scales=fs[:], in_=ils[c][:].rearrange("p o t j -> p (o t j)")
+                    out=fcs[c][:, cols].bitcast(FP8X4),
+                    scales=fss[c][:, cols],
+                    in_=ils[c][:, 4 * h : 4 * h + 4].rearrange("p o t j -> p (o t j)"),
                 )
 
-            def mm2(c):
+            def mm2(c, gi):
                 if c < 0 or c >= NCH:
                     return
-                ps2 = psum.tile([P, 2, NT], F32, name="ps2", tag="ps2", bufs=2)
-                ps2s[c] = ps2
+                if gi == 0:
+                    ps2s[c] = psum.tile([P, 2, NT], F32, name="ps2", tag="ps2", bufs=2)
                 zflat = zcs[c % NZ][:].rearrange("p a b -> p (a b)")
-                for gi in range(2):
-                    for j in range(4):
-                        ol = 4 * gi + j
-                        w0 = 640 * gi + P * j
-                        nc.tensor.matmul_mx(
-                            out=ps2[:, gi, :],
-                            lhsT=zflat[:, w0 : w0 + P].bitcast(FP8X4),
-                            lhsT_scale=css[c][:, P * gi : P * gi + P],
-                            rhs=fcs[c][:, NT * ol : NT * ol + NT].bitcast(FP8X4),
-                            rhs_scale=fss[c][:, NT * ol : NT * ol + NT],
-                            start=(j == 0),
-                            stop=(j == 3),
-                        )
+                for j in range(4):
+                    ol = 4 * gi + j
+                    w0 = 640 * gi + P * j
+                    nc.tensor.matmul_mx(
+                        out=ps2s[c][:, gi, :],
+                        lhsT=zflat[:, w0 : w0 + P].bitcast(FP8X4),
+                        lhsT_scale=css[c][:, P * gi : P * gi + P],
+                        rhs=fcs[c][:, NT * ol : NT * ol + NT].bitcast(FP8X4),
+                        rhs_scale=fss[c][:, NT * ol : NT * ol + NT],
+                        start=(j == 0),
+                        stop=(j == 3),
+                    )
 
             def fin_v(c):
                 if c < 0 or c >= NCH:
                     return
-                tmp = finp.tile([P, 2, NT], F32, name="tmp", tag="tmp")
-                tmps[c] = tmp
+                tmps[c] = finp.tile([P, 2, NT], F32, name="tmp", tag="tmp")
                 for gi in range(2):
                     g = 2 * c + gi
                     nc.vector.scalar_tensor_tensor(
-                        out=tmp[:, gi, :],
+                        out=tmps[c][:, gi, :],
                         in0=ps2s[c][:, gi, :],
                         scalar=sc_t[:, g : g + 1],
                         in1=res_sb[:, g, :],
@@ -310,31 +310,38 @@ def tile_multiscale_gcn_pa_kernel(tc, ada_A, ada_w, ada_b, PA, feat, bn_gamma, b
                     nc.scalar.activation(
                         out=ost[:, gi, :], in_=tmps[c][:, gi, :], func=ACT.Relu, bias=sh_t[:, g : g + 1], scale=1.0
                     )
-                nc.sync.dma_start(out=out_v[:, 2 * c : 2 * c + 2, :], in_=ost[:])
+                queue = nc.sync if c >= NCH - 2 else nc.gpsimd
+                queue.dma_start(out=out_v[:, 2 * c : 2 * c + 2, :], in_=ost[:])
 
             qw(0)
-            il(0)
+            il_s(0)
+            il_v(0)
             for a in range(8):
                 mm1(0, a)
+            bn()
             qw(1)
             ld(3)
-            for c in range(-2, NCH + 2):
+            for c in range(-2, NCH + 1):
                 ld(c + 6)
                 t2(c + 2)
                 k = c + 6
                 if 4 <= k < 4 * NBLK:
                     mm1(k // 4, 2 * (k % 4))
                     mm1(k // 4, 2 * (k % 4) + 1)
-                mm2(c - 1)
                 stt(c + 1)
-                fin_v(c - 2)
+                fin_v(c - 1)
                 qa(c + 1)
                 if c + 1 > 0:
-                    il(c + 1)
+                    il_s(c + 1)
+                qf(c, 0)
+                mm2(c, 0)
+                qf(c, 1)
+                mm2(c, 1)
                 mv(c + 1)
                 if c == -1:
                     qw(2)
                 if c == 1:
                     qw(3)
-                qf(c)
-                fin_s(c - 2)
+                if c + 1 > 0:
+                    il_v(c + 1)
+                fin_s(c - 1)

from contextlib import ExitStack

import concourse.mybir as mybir
from concourse.masks import make_identity

F32 = mybir.dt.float32
BF16 = mybir.dt.bfloat16
I32 = mybir.dt.int32
U8 = mybir.dt.uint8
FP8X4 = mybir.dt.float8_e4m3fn_x4
ALU = mybir.AluOpType
ACT = mybir.ActivationFunctionType

P = 128
NS = 16
NO = 128
NV = 32
NT = 128
EPS = 1e-5
CH = 8
NCH = NO // CH
OB = 32
NBLK = NO // OB
NZ = 4
V_SHARE = (4, 2, 4) * 4 + (2, 2, 2, 4)
MID = F32

FLOPS = 2 * (NS * NO) * 512 * (NV * NV) + 2 * NO * NV * (NS * NV) * NT


def tile_multiscale_gcn_pa_kernel(tc, ada_A, ada_w, ada_b, PA, feat, bn_gamma, bn_beta, bn_mean, bn_var, res, out):
    nc = tc.nc
    with ExitStack() as ctx:
        const = ctx.enter_context(tc.tile_pool(name="const", bufs=1))
        rawp = ctx.enter_context(tc.tile_pool(name="rawp", bufs=6))
        ilp = ctx.enter_context(tc.tile_pool(name="ilp", bufs=3))
        fcp = ctx.enter_context(tc.tile_pool(name="fcp", bufs=6))
        xp = ctx.enter_context(tc.tile_pool(name="xp", bufs=2))
        aip = ctx.enter_context(tc.tile_pool(name="aip", bufs=3))
        finp = ctx.enter_context(tc.tile_pool(name="finp", bufs=4))
        psum = ctx.enter_context(tc.psum_pool(name="psum", bufs=2))
        with tc.manual_schedule():
            zcs = []
            for i in range(NZ):
                z = const.tile([P, CH, 160], I32, name="zc%d" % i, tag="zc%d" % i, align_bytes=64)
                nc.vector.memset(z[:], 0)
                zcs.append(z)
            identF = const.tile([P, P], F32, name="identF", tag="identF")
            make_identity(nc, identF[:])
            identM = identF
            ones = const.tile([P, P], BF16, name="ones", tag="ones")
            nc.gpsimd.memset(ones[:], 1.0)
            bnrow = const.tile([P, 4 * NO], BF16, name="bnrow", tag="bnrow")
            nc.gpsimd.memset(bnrow[:], 0.0)
            warm = const.tile([P, 1], F32, name="warm", tag="warm")
            nc.gpsimd.memset(warm[:], 1.0)
            nc.scalar.activation(out=warm[:], in_=warm[:], func=ACT.Sqrt)

            PAt = const.tile([P, P], BF16, name="PAt", tag="PAt")
            bt = const.tile([P, NO], BF16, name="bt", tag="bt")
            for a in range(8):
                nc.gpsimd.dma_start(
                    out=PAt[a::8, :].rearrange("s (v b) -> s v b", b=4), in_=PA[:, :, 4 * a : 4 * a + 4]
                )
            nc.gpsimd.dma_start(out=bt[:], in_=ada_b.unsqueeze(1).to_broadcast([NS, 8, NO]))
            for k, vec in enumerate((bn_gamma, bn_beta, bn_mean, bn_var)):
                nc.sync.dma_start(out=bnrow[0:1, k * NO : (k + 1) * NO], in_=vec.rearrange("(x o) -> x o", x=1))
            rawA = rawp.tile([P, 4, NV * NV], BF16, name="rawA", tag="raw")
            nc.sync.dma_start(out=rawA[:], in_=ada_A[0].rearrange("(p j) v w -> p j (v w)", j=4))
            rawW = []
            for h in range(2):
                rw = rawp.tile([P, 8, 512], BF16, name="rawW%d" % h, tag="raw")
                rawW.append(rw)
                for q in range(2):
                    s0 = 8 * h + 4 * q
                    nc.sync.dma_start(out=rw[:, 4 * q : 4 * q + 4, :], in_=ada_w[s0 : s0 + 4].rearrange("s o i -> o s i"))

            raws = {}

            def ld(c):
                if c < 0 or c >= NCH:
                    return
                r = rawp.tile([P, CH, 4, NT], BF16, name="raw", tag="raw")
                raws[c] = r
                for ol in range(CH):
                    nc.sync.dma_start(
                        out=r[:, ol].rearrange("p j t -> p (j t)"),
                        in_=feat[:, 0, c * CH + ol].rearrange("s (a j) t -> s a (j t)", j=4),
                    )

            ld(0)
            ld(1)
            ld(2)
            res_sb = const.tile([P, NO // 4, NT], BF16, name="res_sb", tag="res_sb")
            nc.sync.dma_start(out=res_sb[:], in_=res[0].rearrange("(g q) v t -> (q v) g t", q=4))
            out_v = out[0].rearrange("(g q) v t -> (q v) g t", q=4)

            ilA = ilp.tile([P, 8, NV, 4, 4], BF16, name="ilA", tag="il", align_bytes=64)
            rawA_v = rawA[:].rearrange("p j (v a b) -> p a v b j", a=8, b=4)
            for a in range(8):
                if a < 4:
                    nc.vector.tensor_copy(out=ilA[:, a], in_=rawA_v[:, a])
                else:
                    nc.scalar.copy(out=ilA[:, a], in_=rawA_v[:, a])
            acodes = const.tile([P, 1024], I32, name="acodes", tag="acodes", align_bytes=64)
            ascl = const.tile([P, 1024], U8, name="ascl", tag="ascl", align_bytes=64)
            for h in range(2):
                nc.vector.quantize_mx(
                    out=acodes[:, 512 * h : 512 * h + 512].bitcast(FP8X4),
                    scales=ascl[:, 512 * h : 512 * h + 512],
                    in_=ilA[:, 4 * h : 4 * h + 4].rearrange("p a v b j -> p (a v b j)"),
                )

            ilW = const.tile([P, NBLK, NS, OB * 4], BF16, name="ilW", tag="ilW", align_bytes=64)
            ilW_w = ilW[:].bitcast(F32)
            for sp in range(NS // 2):
                tpw = psum.tile([P, 4, P], F32, name="tpw", tag="tp", bufs=4)
                for sl in range(2):
                    s = 2 * sp + sl
                    words = rawW[s // 8][:, s % 8, :].bitcast(F32)
                    for u in range(2):
                        nc.tensor.transpose(tpw[:, 2 * sl + u, :], words[:, u::2], identF[:])
                for sl in range(2):
                    s = 2 * sp + sl
                    dst = ilW_w[:, :, s, :].rearrange("p b (o u) -> p b o u", u=2)
                    src = tpw[:, 2 * sl : 2 * sl + 2, :].rearrange("p u (b o) -> p b o u", b=NBLK)
                    if sp % 2 == 0:
                        nc.scalar.copy(out=dst, in_=src)
                    else:
                        nc.vector.tensor_copy(out=dst, in_=src)
            wcodes = const.tile([P, NS * NO], I32, name="wcodes", tag="wcodes", align_bytes=64)
            wscl = const.tile([P, NS * NO], U8, name="wscl", tag="wscl", align_bytes=64)

            def qw(b):
                nc.vector.quantize_mx(
                    out=wcodes[:, 512 * b : 512 * b + 512].bitcast(FP8X4),
                    scales=wscl[:, 512 * b : 512 * b + 512],
                    in_=ilW[:, b].rearrange("p s x -> p (s x)"),
                )

            sc_t = const.tile([P, NO // 4], F32, name="sc_t", tag="sc_t")
            sh_t = const.tile([P, NO // 4], F32, name="sh_t", tag="sh_t")

            def bn():
                psbn = psum.tile([P, 4 * NO], F32, name="psbn", tag="ps2", bufs=2)
                nc.tensor.matmul(out=psbn[:], lhsT=ones[:], rhs=bnrow[:], start=True, stop=True)
                std = const.tile([P, NO], F32, name="std", tag="std")
                nc.scalar.activation(out=std[:], in_=psbn[:, 3 * NO : 4 * NO], func=ACT.Sqrt, bias=EPS, scale=1.0)
                rstd = const.tile([P, NO], F32, name="rstd", tag="rstd")
                nc.vector.reciprocal(out=rstd[:], in_=std[:])
                scl = const.tile([P, NO], F32, name="scl", tag="scl")
                nc.vector.tensor_tensor(out=scl[:], in0=psbn[:, 0:NO], in1=rstd[:], op=ALU.mult)
                msc = const.tile([P, NO], F32, name="msc", tag="msc")
                nc.vector.tensor_tensor(out=msc[:], in0=psbn[:, 2 * NO : 3 * NO], in1=scl[:], op=ALU.mult)
                shf = const.tile([P, NO], F32, name="shf", tag="shf")
                nc.vector.tensor_tensor(out=shf[:], in0=psbn[:, NO : 2 * NO], in1=msc[:], op=ALU.subtract)
                for q in range(4):
                    rows = slice(32 * q, 32 * q + 32)
                    nc.gpsimd.tensor_copy(out=sc_t[rows, :], in_=scl[rows, q::4])
                    nc.gpsimd.tensor_copy(out=sh_t[rows, :], in_=shf[rows, q::4])

            xs = {}
            tps = {}
            ais = {}
            ccs = {}
            css = {}
            ils = {}
            fcs = {}
            fss = {}
            ps2s = {}
            tmps = {}
            osts = {}

            def mm1(b, a):
                if a == 0:
                    xs[b] = xp.tile([P, NS, 8, OB], MID, name="X", tag="X")
                if b == 0 and a % 2 == 1:
                    ps1 = psum.tile([P, 512], MID, name="ps1b", tag="tp", bufs=4)
                else:
                    ps1 = psum.tile([P, 512], MID, name="ps1", tag="ps1", bufs=2)
                nc.tensor.matmul_mx(
                    out=ps1[:],
                    lhsT=acodes[:, P * a : P * a + P].bitcast(FP8X4),
                    lhsT_scale=ascl[:, P * a : P * a + P],
                    rhs=wcodes[:, 512 * b : 512 * b + 512].bitcast(FP8X4),
                    rhs_scale=wscl[:, 512 * b : 512 * b + 512],
                    start=True,
                    stop=True,
                )
                if b == 0 and a % 2 == 1:
                    nc.vector.tensor_copy(out=xs[b][:, :, a, :], in_=ps1[:].rearrange("p (s o) -> p s o", o=OB))
                else:
                    nc.scalar.copy(out=xs[b][:, :, a, :], in_=ps1[:].rearrange("p (s o) -> p s o", o=OB))

            def t2(c):
                if c < 0 or c >= NCH:
                    return
                xv = xs[c // 4][:].rearrange("p s a o -> p (s a) o")
                tps[c] = []
                for h in range(2):
                    tp = psum.tile([P, 4, P], MID, name="tp", tag="tp", bufs=4)
                    tps[c].append(tp)
                    for i in range(4):
                        nc.tensor.transpose(tp[:, i, :], xv[:, :, (c % 4) * CH + 4 * h + i], identM[:])

            def stt(c):
                if c < 0 or c >= NCH:
                    return
                ai = aip.tile([P, CH * P], BF16, name="ai", tag="ai", bufs=3, align_bytes=64)
                ais[c] = ai
                for i in range(CH):
                    o = c * CH + i
                    nc.vector.scalar_tensor_tensor(
                        out=ai[:, P * i : P * i + P],
                        in0=tps[c][i // 4][:, i % 4, :],
                        scalar=bt[:, o : o + 1],
                        in1=PAt[:],
                        op0=ALU.add,
                        op1=ALU.mult,
                    )

            def qa(c):
                if c < 0 or c >= NCH:
                    return
                cc = aip.tile([P, CH * NV], I32, name="cc", tag="cc", bufs=3, align_bytes=64)
                cs = aip.tile([P, CH * NV], U8, name="cs", tag="cs", bufs=5, align_bytes=64)
                ccs[c] = cc
                css[c] = cs
                nc.vector.quantize_mx(out=cc[:].bitcast(FP8X4), scales=cs[:], in_=ais[c][:])

            def mv(c):
                if c < 0 or c >= NCH:
                    return
                nc.vector.tensor_copy(out=zcs[c % NZ][:, :, 0:NV], in_=ccs[c][:].rearrange("p (a b) -> p a b", b=NV))

            def cuts(c, lo, hi):
                if c == NCH - 1:
                    mid = (lo + hi) // 2
                    return [(lo, mid), (mid, hi)]
                return [(lo, hi)]

            def il_s(c):
                if c < 0 or c >= NCH:
                    return
                ils[c] = ilp.tile([P, CH, NT, 4], BF16, name="il", tag="il", align_bytes=64)
                src = raws[c][:].rearrange("p o j t -> p o t j")
                for lo, hi in cuts(c, 0, CH - V_SHARE[c]):
                    nc.scalar.copy(out=ils[c][:, lo:hi], in_=src[:, lo:hi])

            def il_v(c):
                if c < 0 or c >= NCH:
                    return
                src = raws[c][:].rearrange("p o j t -> p o t j")
                for lo, hi in cuts(c, CH - V_SHARE[c], CH):
                    nc.vector.tensor_copy(out=ils[c][:, lo:hi], in_=src[:, lo:hi])

            def qf(c, h):
                if c < 0 or c >= NCH:
                    return
                if h == 0:
                    fcs[c] = fcp.tile([P, CH * NT], I32, name="fc", tag="fc", align_bytes=64)
                    fss[c] = fcp.tile([P, CH * NT], U8, name="fs", tag="fs", align_bytes=64)
                cols = slice(512 * h, 512 * h + 512)
                nc.vector.quantize_mx(
                    out=fcs[c][:, cols].bitcast(FP8X4),
                    scales=fss[c][:, cols],
                    in_=ils[c][:, 4 * h : 4 * h + 4].rearrange("p o t j -> p (o t j)"),
                )

            def mm2(c, gi):
                if c < 0 or c >= NCH:
                    return
                if gi == 0:
                    ps2s[c] = psum.tile([P, 2, NT], F32, name="ps2", tag="ps2", bufs=2)
                zflat = zcs[c % NZ][:].rearrange("p a b -> p (a b)")
                for j in range(4):
                    ol = 4 * gi + j
                    w0 = 640 * gi + P * j
                    nc.tensor.matmul_mx(
                        out=ps2s[c][:, gi, :],
                        lhsT=zflat[:, w0 : w0 + P].bitcast(FP8X4),
                        lhsT_scale=css[c][:, P * gi : P * gi + P],
                        rhs=fcs[c][:, NT * ol : NT * ol + NT].bitcast(FP8X4),
                        rhs_scale=fss[c][:, NT * ol : NT * ol + NT],
                        start=(j == 0),
                        stop=(j == 3),
                    )

            def fin_v(c):
                if c < 0 or c >= NCH:
                    return
                tmps[c] = finp.tile([P, 2, NT], F32, name="tmp", tag="tmp")
                for gi in range(2):
                    g = 2 * c + gi
                    nc.vector.scalar_tensor_tensor(
                        out=tmps[c][:, gi, :],
                        in0=ps2s[c][:, gi, :],
                        scalar=sc_t[:, g : g + 1],
                        in1=res_sb[:, g, :],
                        op0=ALU.mult,
                        op1=ALU.add,
                    )

            def fin_s(c):
                if c < 0 or c >= NCH:
                    return
                ost = finp.tile([P, 2, NT], F32, name="ost", tag="ost")
                for gi in range(2):
                    g = 2 * c + gi
                    nc.scalar.activation(
                        out=ost[:, gi, :], in_=tmps[c][:, gi, :], func=ACT.Relu, bias=sh_t[:, g : g + 1], scale=1.0
                    )
                queue = nc.sync if c >= NCH - 2 else nc.gpsimd
                queue.dma_start(out=out_v[:, 2 * c : 2 * c + 2, :], in_=ost[:])

            qw(0)
            il_s(0)
            il_v(0)
            for a in range(8):
                mm1(0, a)
            bn()
            qw(1)
            ld(3)
            for c in range(-2, NCH + 1):
                ld(c + 6)
                t2(c + 2)
                k = c + 6
                if 4 <= k < 4 * NBLK:
                    mm1(k // 4, 2 * (k % 4))
                    mm1(k // 4, 2 * (k % 4) + 1)
                stt(c + 1)
                fin_v(c - 1)
                qa(c + 1)
                if c + 1 > 0:
                    il_s(c + 1)
                qf(c, 0)
                mm2(c, 0)
                qf(c, 1)
                mm2(c, 1)
                mv(c + 1)
                if c == -1:
                    qw(2)
                if c == 1:
                    qw(3)
                if c + 1 > 0:
                    il_v(c + 1)
                fin_s(c - 1)
